import numpy as np
import ml_dtypes


def mxq(x, axis, fmt="e4m3"):
    dtype, down = {"e4m3": (ml_dtypes.float8_e4m3fn, 7), "e5m2": (ml_dtypes.float8_e5m2, 14)}[fmt]
    v = np.moveaxis(np.asarray(x, np.float32).astype(ml_dtypes.bfloat16).astype(np.float64), axis, -1)
    blocks = v.reshape(v.shape[:-1] + (-1, 32))
    amax = np.abs(blocks).max(-1, keepdims=True)
    byte = np.maximum(np.where(amax > 0, np.frexp(amax)[1] - 1 + 127, 0) - down, 1)
    scale = np.exp2(byte - 127.0)
    codes = (blocks / scale).astype(np.float32).astype(dtype).astype(np.float64)
    return np.moveaxis((codes * scale).reshape(v.shape), -1, axis)


WIDE = False


def mx_kscale(k):
    if not WIDE:
        return np.ones(k)
    levels = np.array([10, -10, 5, -5, 0])
    a = np.random.permutation(np.resize(levels, k // 512 * 4)).reshape(k // 512, 4)
    idx = np.arange(k)
    return np.exp2(a[idx // 512, idx % 128 // 32])


BF16 = ml_dtypes.bfloat16


def bf(x):
    return np.asarray(x, np.float32).astype(BF16)


def f64(x):
    return np.asarray(x).astype(np.float64)


B, D, C = 4096, 32, 1024
EPS_SQRT = 1e-10
EPS_NORM = 1e-12


def setup_inputs():
    s = mx_kscale(D * D)
    a = np.round(np.log2(np.array([s.max(), s.min()])) / 2)
    r = np.repeat(np.exp2(a - a.min()), D // 2)
    g = np.exp2(np.round(np.log2(np.mean(r ** 2))))
    return {"feat": bf(np.random.standard_normal((B, D)) * r ** 2),
            "W": bf(np.random.standard_normal((C, D * D)) * g / np.outer(r, r).reshape(-1)),
            "b": bf(np.random.standard_normal(C) * 0.3)}


def reference(feat, W, b):
    feat = f64(feat)
    x = (feat[:, :, None] * feat[:, None, :]).reshape(feat.shape[0], -1)
    x = np.sign(x) * np.sqrt(np.abs(x) + EPS_SQRT)
    norm = np.maximum(np.linalg.norm(x, axis=1, keepdims=True), EPS_NORM)
    x = x / norm
    return (mxq(x, 1, "e4m3") @ mxq(f64(W), 1, "e4m3").T) + f64(b)

@@ -1,0 +1,237 @@
+from contextlib import ExitStack
+
+import concourse.mybir as mybir
+from concourse.masks import make_identity
+
+F32 = mybir.dt.float32
+BF16 = mybir.dt.bfloat16
+U32 = mybir.dt.uint32
+U8 = mybir.dt.uint8
+FP8X4 = mybir.dt.float8_e4m3fn_x4
+ALU = mybir.AluOpType
+ACTF = mybir.ActivationFunctionType
+AX = mybir.AxisListType
+
+P = 128
+B, D, C = 4096, 32, 1024
+K = D * D
+NT = B // P
+EPS_SQRT = 1e-10
+EPS_NORM = 1e-12
+FLOPS = 2 * B * K * C
+
+
+def tile_bcnnresnet_t_kernel(tc, feat, W, b, out):
+    nc = tc.nc
+    with ExitStack() as ctx:
+        keep = ctx.enter_context(tc.tile_pool(name="keep", bufs=1))
+        qpool = ctx.enter_context(tc.tile_pool(name="qpool", bufs=4))
+        xpool = ctx.enter_context(tc.tile_pool(name="xpool", bufs=6))
+        gpool = ctx.enter_context(tc.tile_pool(name="gpool", bufs=4))
+        cpool = ctx.enter_context(tc.tile_pool(name="cpool", bufs=4))
+        opool = ctx.enter_context(tc.tile_pool(name="opool", bufs=4))
+        ps_t = ctx.enter_context(tc.psum_pool(name="ps_t", bufs=3))
+        ps_o = ctx.enter_context(tc.psum_pool(name="ps_o", bufs=5))
+
+        f_sb = keep.tile([P, NT * D], BF16)
+        nc.sync.dma_start(out=f_sb[:], in_=feat.rearrange("(p t) d -> p (t d)", t=NT))
+        w_raw = keep.tile([P, 8 * K], BF16)
+        w_view = W.rearrange("(ct p) k -> p ct k", p=P)
+        for g in range(4):
+            nc.sync.dma_start(
+                out=w_raw[:, 2 * g * K : (2 * g + 2) * K].rearrange("p (ct k) -> p ct k", ct=2),
+                in_=w_view[:, 2 * g : 2 * g + 2, :],
+            )
+        bias_bf = keep.tile([P, C], BF16)
+        nc.sync.dma_start(out=bias_bf[:], in_=b.partition_broadcast(P))
+
+        ident_bf = keep.tile([P, P], BF16)
+        make_identity(nc, ident_bf[:])
+        ident_f = keep.tile([P, P], F32)
+        make_identity(nc, ident_f[:])
+
+        a_nat = keep.tile([P, NT * D], BF16)
+        nc.scalar.activation(out=a_nat[:], in_=f_sb[:], func=ACTF.Abs)
+        s_nat = keep.tile([P, NT * D], BF16)
+        nc.scalar.activation(out=s_nat[:], in_=f_sb[:], func=ACTF.Sign)
+        a_per = keep.tile([P, NT * D], BF16)
+        nc.vector.tensor_copy(
+            out=a_per[:].rearrange("p (m e r) -> p m e r", e=2, r=8),
+            in_=a_nat[:].rearrange("p (m r e) -> p m e r", e=2, r=8),
+        )
+        sum_a = keep.tile([P, NT], F32)
+        nc.vector.tensor_reduce(
+            out=sum_a[:], in_=a_nat[:].rearrange("p (t d) -> p t d", d=D), axis=AX.X, op=ALU.add
+        )
+        nz = keep.tile([P, NT * D], BF16)
+        nc.vector.tensor_tensor(out=nz[:], in0=s_nat[:], in1=s_nat[:], op=ALU.mult)
+        cnt = keep.tile([P, NT], F32)
+        nc.vector.tensor_reduce(
+            out=cnt[:], in_=nz[:].rearrange("p (t d) -> p t d", d=D), axis=AX.X, op=ALU.add
+        )
+        sq_a = keep.tile([P, NT], F32)
+        nc.vector.tensor_tensor(out=sq_a[:], in0=sum_a[:], in1=sum_a[:], op=ALU.mult)
+        sq_c = keep.tile([P, NT], F32)
+        nc.vector.tensor_tensor(out=sq_c[:], in0=cnt[:], in1=cnt[:], op=ALU.mult)
+        n2 = keep.tile([P, NT], F32)
+        nc.vector.scalar_tensor_tensor(
+            out=n2[:], in0=sq_c[:], scalar=EPS_SQRT, in1=sq_a[:], op0=ALU.mult, op1=ALU.add
+        )
+        n2c = keep.tile([P, NT], F32)
+        nc.vector.tensor_scalar_max(out=n2c[:], in0=n2[:], scalar1=EPS_NORM * EPS_NORM)
+        rho = keep.tile([P, NT], F32)
+        nc.vector.reciprocal(out=rho[:], in_=n2c[:])
+        erho = keep.tile([P, NT], F32)
+        nc.vector.tensor_scalar_mul(out=erho[:], in0=rho[:], scalar1=EPS_SQRT)
+        s_per = keep.tile([P, NT * D], BF16)
+        nc.vector.tensor_copy(
+            out=s_per[:].rearrange("p (m e r) -> p m e r", e=2, r=8),
+            in_=s_nat[:].rearrange("p (m r e) -> p m e r", e=2, r=8),
+        )
+        s_rep = keep.tile([P, NT * D * 8], BF16)
+        nc.vector.tensor_copy(
+            out=s_rep[:].rearrange("p (m r) -> p m r", r=8),
+            in_=s_nat[:].unsqueeze(2).to_broadcast([P, NT * D, 8]),
+        )
+        bias32 = keep.tile([P, C], F32)
+        nc.vector.tensor_copy(out=bias32[:], in_=bias_bf[:])
+
+        w_ord = keep.tile([P, 8 * K], BF16)
+        w_grp = keep.tile([P, 2 * C * 4], BF16, align_bytes=64)
+        w_cod = keep.tile([P, 2 * C], U32, align_bytes=64)
+        w_scl = keep.tile([P, 2 * C], U8, align_bytes=64)
+        raw_w = w_raw[:].bitcast(F32)
+        ord_w = w_ord[:].bitcast(F32)
+        grp_w = w_grp[:].bitcast(F32).rearrange("p (c n u) -> p c n u", c=2, u=2)
+        for ct in range(8):
+            for c in range(2):
+                lo = ct * 512 + c * 256
+                nc.scalar.copy(
+                    out=ord_w[:, lo : lo + 256].rearrange("p (u q r) -> p u q r", u=2, r=8),
+                    in_=raw_w[:, lo : lo + 256].rearrange("p (q u r) -> p u q r", u=2, r=8),
+                )
+            wt = ps_t.tile([P, 4, P], F32, tag="tp")
+            for s in range(4):
+                lo = ct * 512 + s * 128
+                nc.tensor.transpose(out=wt[:, s, :], in_=ord_w[:, lo : lo + 128], identity=ident_f[:])
+            nc.scalar.copy(
+                out=grp_w[:, :, ct * P : (ct + 1) * P, :],
+                in_=wt[:].rearrange("p (c u) n -> p c n u", c=2),
+            )
+            if ct % 4 == 3:
+                h = ct // 4
+                for c in range(2):
+                    lo = c * C + h * 512
+                    nc.vector.quantize_mx(
+                        out=w_cod[:, lo : lo + 512].bitcast(FP8X4),
+                        scales=w_scl[:, lo : lo + 512],
+                        in_=w_grp[:, 4 * lo : 4 * lo + 2048],
+                    )
+
+        out_v = out.rearrange("(p t) c -> p t c", t=NT)
+        o_sb = None
+        for k in range(NT):
+            fo = k * D
+            q32 = qpool.tile([P, 768], F32)
+            nc.gpsimd.tensor_tensor(
+                out=q32[:, 0:512].rearrange("p (w q r) -> p w q r", w=4, r=8),
+                in0=a_nat[:, fo : fo + 16].unsqueeze(1).unsqueeze(3).to_broadcast([P, 4, 16, 8]),
+                in1=a_per[:, fo : fo + 32]
+                .rearrange("p (w r) -> p w r", r=8)
+                .unsqueeze(2)
+                .to_broadcast([P, 4, 16, 8]),
+                op=ALU.mult,
+            )
+            nc.gpsimd.tensor_tensor(
+                out=q32[:, 512:768].rearrange("p (w q r) -> p w q r", w=2, r=8),
+                in0=a_nat[:, fo + 16 : fo + 32].unsqueeze(1).unsqueeze(3).to_broadcast([P, 2, 16, 8]),
+                in1=a_per[:, fo + 16 : fo + 32]
+                .rearrange("p (w r) -> p w r", r=8)
+                .unsqueeze(2)
+                .to_broadcast([P, 2, 16, 8]),
+                op=ALU.mult,
+            )
+            xf = xpool.tile([P, K], BF16)
+            nc.scalar.activation(
+                out=xf[:, 0:768],
+                in_=q32[:],
+                func=ACTF.Sqrt,
+                bias=erho[:, k : k + 1],
+                scale=rho[:, k : k + 1],
+            )
+            nc.vector.tensor_tensor(
+                out=xf[:, 0:512].rearrange("p (w q r) -> p w q r", w=4, r=8),
+                in0=xf[:, 0:512].rearrange("p (w q r) -> p w q r", w=4, r=8),
+                in1=s_per[:, fo : fo + 32]
+                .rearrange("p (w r) -> p w r", r=8)
+                .unsqueeze(2)
+                .to_broadcast([P, 4, 16, 8]),
+                op=ALU.mult,
+            )
+            nc.vector.tensor_tensor(
+                out=xf[:, 512:768].rearrange("p (w q r) -> p w q r", w=2, r=8),
+                in0=xf[:, 512:768].rearrange("p (w q r) -> p w q r", w=2, r=8),
+                in1=s_per[:, fo + 16 : fo + 32]
+                .rearrange("p (w r) -> p w r", r=8)
+                .unsqueeze(2)
+                .to_broadcast([P, 2, 16, 8]),
+                op=ALU.mult,
+            )
+            nc.vector.tensor_tensor(
+                out=xf[:, 0:512].rearrange("p (w m) -> p w m", w=4),
+                in0=xf[:, 0:512].rearrange("p (w m) -> p w m", w=4),
+                in1=s_rep[:, fo * 8 : fo * 8 + 128].unsqueeze(1).to_broadcast([P, 4, 128]),
+                op=ALU.mult,
+            )
+            nc.vector.tensor_tensor(
+                out=xf[:, 512:768].rearrange("p (w m) -> p w m", w=2),
+                in0=xf[:, 512:768].rearrange("p (w m) -> p w m", w=2),
+                in1=s_rep[:, fo * 8 + 128 : fo * 8 + 256].unsqueeze(1).to_broadcast([P, 2, 128]),
+                op=ALU.mult,
+            )
+            for eb in range(2):
+                nc.scalar.copy(
+                    out=xf[:, 768 + 128 * eb : 896 + 128 * eb].rearrange(
+                        "p (ra ea rb) -> p ra ea rb", ra=8, ea=2
+                    ),
+                    in_=xf[:, 256:512]
+                    .rearrange("p (ea rb eb ra) -> p eb ra ea rb", ea=2, rb=8, eb=2)[:, eb],
+                )
+            xt = ps_t.tile([P, 8, P], BF16, tag="tp")
+            for c, u, z in ((0, 0, 0), (0, 1, 1), (1, 0, 3), (1, 1, 2)):
+                for e in range(2):
+                    lo = z * 256 + e * 128
+                    nc.tensor.transpose(
+                        out=xt[:, 4 * c + 2 * u + e, :], in_=xf[:, lo : lo + 128], identity=ident_bf[:]
+                    )
+            grp = gpool.tile([P, K], BF16, align_bytes=64)
+            nc.scalar.copy(
+                out=grp[:].rearrange("p (c n t) -> p c n t", c=2, t=4),
+                in_=xt[:].rearrange("p (c t) n -> p c n t", c=2),
+            )
+            x_cod = cpool.tile([P, 256], U32, align_bytes=64)
+            x_scl = cpool.tile([P, 256], U8, align_bytes=64)
+            nc.vector.quantize_mx(out=x_cod[:].bitcast(FP8X4), scales=x_scl[:], in_=grp[:])
+            if k % 2 == 0:
+                o_sb = opool.tile([P, 2, C], F32)
+            for h in range(2):
+                acc = ps_o.tile([P, 512], F32)
+                for c in range(2):
+                    lo = c * C + h * 512
+                    nc.tensor.matmul_mx(
+                        out=acc[:],
+                        lhsT=x_cod[:, c * P : (c + 1) * P].bitcast(FP8X4),
+                        lhsT_scale=x_scl[:, c * P : (c + 1) * P],
+                        rhs=w_cod[:, lo : lo + 512].bitcast(FP8X4),
+                        rhs_scale=w_scl[:, lo : lo + 512],
+                        start=(c == 0),
+                        stop=(c == 1),
+                    )
+                nc.vector.tensor_tensor(
+                    out=o_sb[:, k % 2, h * 512 : (h + 1) * 512],
+                    in0=acc[:],
+                    in1=bias32[:, h * 512 : (h + 1) * 512],
+                    op=ALU.add,
+                )
+            if k % 2 == 1:
+                nc.sync.dma_start(out=out_v[:, k - 1 : k + 1, :], in_=o_sb[:])

@@ -27,11 +27,12 @@ def tile_bcnnresnet_t_kernel(tc, feat, W, b, out):
         keep = ctx.enter_context(tc.tile_pool(name="keep", bufs=1))
         qpool = ctx.enter_context(tc.tile_pool(name="qpool", bufs=4))
         xpool = ctx.enter_context(tc.tile_pool(name="xpool", bufs=6))
-        gpool = ctx.enter_context(tc.tile_pool(name="gpool", bufs=4))
-        cpool = ctx.enter_context(tc.tile_pool(name="cpool", bufs=4))
+        gpool = ctx.enter_context(tc.tile_pool(name="gpool", bufs=3))
+        cpool = ctx.enter_context(tc.tile_pool(name="cpool", bufs=3))
         opool = ctx.enter_context(tc.tile_pool(name="opool", bufs=4))
-        ps_t = ctx.enter_context(tc.psum_pool(name="ps_t", bufs=3))
-        ps_o = ctx.enter_context(tc.psum_pool(name="ps_o", bufs=5))
+        ps_t = ctx.enter_context(tc.psum_pool(name="ps_t", bufs=2))
+        ps_s = ctx.enter_context(tc.psum_pool(name="ps_s", bufs=2))
+        ps_o = ctx.enter_context(tc.psum_pool(name="ps_o", bufs=4))
 
         f_sb = keep.tile([P, NT * D], BF16)
         nc.sync.dma_start(out=f_sb[:], in_=feat.rearrange("(p t) d -> p (t d)", t=NT))
@@ -50,21 +51,33 @@ def tile_bcnnresnet_t_kernel(tc, feat, W, b, out):
         ident_f = keep.tile([P, P], F32)
         make_identity(nc, ident_f[:])
 
+        sel_rep = keep.tile([P, P * 8], BF16)
+        nc.vector.tensor_copy(
+            out=sel_rep[:].rearrange("p (m r) -> p m r", r=8),
+            in_=ident_bf[:].unsqueeze(2).to_broadcast([P, P, 8]),
+        )
+        sel_per = keep.tile([P, P], BF16)
+        nc.vector.tensor_copy(
+            out=sel_per[:].rearrange("p (m e r) -> p m e r", e=2, r=8),
+            in_=ident_bf[:].rearrange("p (m r e) -> p m e r", e=2, r=8),
+        )
+
         a_nat = keep.tile([P, NT * D], BF16)
         nc.scalar.activation(out=a_nat[:], in_=f_sb[:], func=ACTF.Abs)
         s_nat = keep.tile([P, NT * D], BF16)
         nc.scalar.activation(out=s_nat[:], in_=f_sb[:], func=ACTF.Sign)
         a_per = keep.tile([P, NT * D], BF16)
-        nc.vector.tensor_copy(
+        nc.scalar.activation(
             out=a_per[:].rearrange("p (m e r) -> p m e r", e=2, r=8),
-            in_=a_nat[:].rearrange("p (m r e) -> p m e r", e=2, r=8),
+            in_=f_sb[:].rearrange("p (m r e) -> p m e r", e=2, r=8),
+            func=ACTF.Abs,
         )
+        nz = keep.tile([P, NT * D], BF16)
+        nc.scalar.activation(out=nz[:], in_=s_nat[:], func=ACTF.Abs)
         sum_a = keep.tile([P, NT], F32)
         nc.vector.tensor_reduce(
             out=sum_a[:], in_=a_nat[:].rearrange("p (t d) -> p t d", d=D), axis=AX.X, op=ALU.add
         )
-        nz = keep.tile([P, NT * D], BF16)
-        nc.vector.tensor_tensor(out=nz[:], in0=s_nat[:], in1=s_nat[:], op=ALU.mult)
         cnt = keep.tile([P, NT], F32)
         nc.vector.tensor_reduce(
             out=cnt[:], in_=nz[:].rearrange("p (t d) -> p t d", d=D), axis=AX.X, op=ALU.add
@@ -83,18 +96,11 @@ def tile_bcnnresnet_t_kernel(tc, feat, W, b, out):
         nc.vector.reciprocal(out=rho[:], in_=n2c[:])
         erho = keep.tile([P, NT], F32)
         nc.vector.tensor_scalar_mul(out=erho[:], in0=rho[:], scalar1=EPS_SQRT)
-        s_per = keep.tile([P, NT * D], BF16)
-        nc.vector.tensor_copy(
-            out=s_per[:].rearrange("p (m e r) -> p m e r", e=2, r=8),
-            in_=s_nat[:].rearrange("p (m r e) -> p m e r", e=2, r=8),
-        )
-        s_rep = keep.tile([P, NT * D * 8], BF16)
-        nc.vector.tensor_copy(
-            out=s_rep[:].rearrange("p (m r) -> p m r", r=8),
-            in_=s_nat[:].unsqueeze(2).to_broadcast([P, NT * D, 8]),
-        )
-        bias32 = keep.tile([P, C], F32)
-        nc.vector.tensor_copy(out=bias32[:], in_=bias_bf[:])
+        st_ps = ps_t.tile([P, 8, P], BF16, tag="tp")
+        for g in range(8):
+            nc.tensor.transpose(out=st_ps[:, g, :], in_=s_nat[:, g * P : (g + 1) * P], identity=ident_bf[:])
+        s_t = keep.tile([P, 8, P], BF16)
+        nc.scalar.copy(out=s_t[:], in_=st_ps[:])
 
         w_ord = keep.tile([P, 8 * K], BF16)
         w_grp = keep.tile([P, 2 * C * 4], BF16, align_bytes=64)
@@ -129,109 +135,120 @@ def tile_bcnnresnet_t_kernel(tc, feat, W, b, out):
                     )
 
         out_v = out.rearrange("(p t) c -> p t c", t=NT)
-        o_sb = None
-        for k in range(NT):
-            fo = k * D
-            q32 = qpool.tile([P, 768], F32)
-            nc.gpsimd.tensor_tensor(
-                out=q32[:, 0:512].rearrange("p (w q r) -> p w q r", w=4, r=8),
-                in0=a_nat[:, fo : fo + 16].unsqueeze(1).unsqueeze(3).to_broadcast([P, 4, 16, 8]),
-                in1=a_per[:, fo : fo + 32]
-                .rearrange("p (w r) -> p w r", r=8)
-                .unsqueeze(2)
-                .to_broadcast([P, 4, 16, 8]),
-                op=ALU.mult,
+        for kp in range(NT // 2):
+            g, hh = kp // 2, kp % 2
+            sg = ps_s.tile([P, 1024], BF16)
+            nc.tensor.matmul(
+                out=sg[:, 0:512], lhsT=s_t[:, g, :], rhs=sel_rep[:, hh * 512 : (hh + 1) * 512], start=True, stop=True
             )
-            nc.gpsimd.tensor_tensor(
-                out=q32[:, 512:768].rearrange("p (w q r) -> p w q r", w=2, r=8),
-                in0=a_nat[:, fo + 16 : fo + 32].unsqueeze(1).unsqueeze(3).to_broadcast([P, 2, 16, 8]),
-                in1=a_per[:, fo + 16 : fo + 32]
-                .rearrange("p (w r) -> p w r", r=8)
-                .unsqueeze(2)
-                .to_broadcast([P, 2, 16, 8]),
-                op=ALU.mult,
+            nc.tensor.matmul(
+                out=sg[:, 512:576], lhsT=s_t[:, g, :], rhs=sel_per[:, hh * 64 : (hh + 1) * 64], start=True, stop=True
             )
-            xf = xpool.tile([P, K], BF16)
-            nc.scalar.activation(
-                out=xf[:, 0:768],
-                in_=q32[:],
-                func=ACTF.Sqrt,
-                bias=erho[:, k : k + 1],
-                scale=rho[:, k : k + 1],
-            )
-            nc.vector.tensor_tensor(
-                out=xf[:, 0:512].rearrange("p (w q r) -> p w q r", w=4, r=8),
-                in0=xf[:, 0:512].rearrange("p (w q r) -> p w q r", w=4, r=8),
-                in1=s_per[:, fo : fo + 32]
-                .rearrange("p (w r) -> p w r", r=8)
-                .unsqueeze(2)
-                .to_broadcast([P, 4, 16, 8]),
-                op=ALU.mult,
-            )
-            nc.vector.tensor_tensor(
-                out=xf[:, 512:768].rearrange("p (w q r) -> p w q r", w=2, r=8),
-                in0=xf[:, 512:768].rearrange("p (w q r) -> p w q r", w=2, r=8),
-                in1=s_per[:, fo + 16 : fo + 32]
-                .rearrange("p (w r) -> p w r", r=8)
-                .unsqueeze(2)
-                .to_broadcast([P, 2, 16, 8]),
-                op=ALU.mult,
-            )
-            nc.vector.tensor_tensor(
-                out=xf[:, 0:512].rearrange("p (w m) -> p w m", w=4),
-                in0=xf[:, 0:512].rearrange("p (w m) -> p w m", w=4),
-                in1=s_rep[:, fo * 8 : fo * 8 + 128].unsqueeze(1).to_broadcast([P, 4, 128]),
-                op=ALU.mult,
-            )
-            nc.vector.tensor_tensor(
-                out=xf[:, 512:768].rearrange("p (w m) -> p w m", w=2),
-                in0=xf[:, 512:768].rearrange("p (w m) -> p w m", w=2),
-                in1=s_rep[:, fo * 8 + 128 : fo * 8 + 256].unsqueeze(1).to_broadcast([P, 2, 128]),
-                op=ALU.mult,
-            )
-            for eb in range(2):
-                nc.scalar.copy(
-                    out=xf[:, 768 + 128 * eb : 896 + 128 * eb].rearrange(
-                        "p (ra ea rb) -> p ra ea rb", ra=8, ea=2
-                    ),
-                    in_=xf[:, 256:512]
-                    .rearrange("p (ea rb eb ra) -> p eb ra ea rb", ea=2, rb=8, eb=2)[:, eb],
+            grp = gpool.tile([P, 2 * K], BF16, align_bytes=64)
+            for kk in range(2):
+                k = 2 * kp + kk
+                fo = k * D
+                q32 = qpool.tile([P, 768], F32)
+                nc.gpsimd.tensor_tensor(
+                    out=q32[:, 0:512].rearrange("p (w q r) -> p w q r", w=4, r=8),
+                    in0=a_nat[:, fo : fo + 16].unsqueeze(1).unsqueeze(3).to_broadcast([P, 4, 16, 8]),
+                    in1=a_per[:, fo : fo + 32]
+                    .rearrange("p (w r) -> p w r", r=8)
+                    .unsqueeze(2)
+                    .to_broadcast([P, 4, 16, 8]),
+                    op=ALU.mult,
                 )
-            xt = ps_t.tile([P, 8, P], BF16, tag="tp")
-            for c, u, z in ((0, 0, 0), (0, 1, 1), (1, 0, 3), (1, 1, 2)):
-                for e in range(2):
-                    lo = z * 256 + e * 128
-                    nc.tensor.transpose(
-                        out=xt[:, 4 * c + 2 * u + e, :], in_=xf[:, lo : lo + 128], identity=ident_bf[:]
-                    )
-            grp = gpool.tile([P, K], BF16, align_bytes=64)
-            nc.scalar.copy(
-                out=grp[:].rearrange("p (c n t) -> p c n t", c=2, t=4),
-                in_=xt[:].rearrange("p (c t) n -> p c n t", c=2),
-            )
-            x_cod = cpool.tile([P, 256], U32, align_bytes=64)
-            x_scl = cpool.tile([P, 256], U8, align_bytes=64)
-            nc.vector.quantize_mx(out=x_cod[:].bitcast(FP8X4), scales=x_scl[:], in_=grp[:])
-            if k % 2 == 0:
-                o_sb = opool.tile([P, 2, C], F32)
-            for h in range(2):
-                acc = ps_o.tile([P, 512], F32)
-                for c in range(2):
-                    lo = c * C + h * 512
-                    nc.tensor.matmul_mx(
-                        out=acc[:],
-                        lhsT=x_cod[:, c * P : (c + 1) * P].bitcast(FP8X4),
-                        lhsT_scale=x_scl[:, c * P : (c + 1) * P],
-                        rhs=w_cod[:, lo : lo + 512].bitcast(FP8X4),
-                        rhs_scale=w_scl[:, lo : lo + 512],
-                        start=(c == 0),
-                        stop=(c == 1),
-                    )
+                nc.gpsimd.tensor_tensor(
+                    out=q32[:, 512:768].rearrange("p (w q r) -> p w q r", w=2, r=8),
+                    in0=a_nat[:, fo + 16 : fo + 32].unsqueeze(1).unsqueeze(3).to_broadcast([P, 2, 16, 8]),
+                    in1=a_per[:, fo + 16 : fo + 32]
+                    .rearrange("p (w r) -> p w r", r=8)
+                    .unsqueeze(2)
+                    .to_broadcast([P, 2, 16, 8]),
+                    op=ALU.mult,
+                )
+                xf = xpool.tile([P, K], BF16)
+                nc.scalar.activation(
+                    out=xf[:, 0:768],
+                    in_=q32[:],
+                    func=ACTF.Sqrt,
+                    bias=erho[:, k : k + 1],
+                    scale=rho[:, k : k + 1],
+                )
+                so = 512 + kk * 32
+                ro = kk * 256
                 nc.vector.tensor_tensor(
-                    out=o_sb[:, k % 2, h * 512 : (h + 1) * 512],
-                    in0=acc[:],
-                    in1=bias32[:, h * 512 : (h + 1) * 512],
-                    op=ALU.add,
+                    out=xf[:, 0:512].rearrange("p (w q r) -> p w q r", w=4, r=8),
+                    in0=xf[:, 0:512].rearrange("p (w q r) -> p w q r", w=4, r=8),
+                    in1=sg[:, so : so + 32]
+                    .rearrange("p (w r) -> p w r", r=8)
+                    .unsqueeze(2)
+                    .to_broadcast([P, 4, 16, 8]),
+                    op=ALU.mult,
                 )
-            if k % 2 == 1:
-                nc.sync.dma_start(out=out_v[:, k - 1 : k + 1, :], in_=o_sb[:])
+                nc.vector.tensor_tensor(
+                    out=xf[:, 512:768].rearrange("p (w q r) -> p w q r", w=2, r=8),
+                    in0=xf[:, 512:768].rearrange("p (w q r) -> p w q r", w=2, r=8),
+                    in1=sg[:, so + 16 : so + 32]
+                    .rearrange("p (w r) -> p w r", r=8)
+                    .unsqueeze(2)
+                    .to_broadcast([P, 2, 16, 8]),
+                    op=ALU.mult,
+                )
+                nc.vector.tensor_tensor(
+                    out=xf[:, 0:512].rearrange("p (w m) -> p w m", w=4),
+                    in0=xf[:, 0:512].rearrange("p (w m) -> p w m", w=4),
+                    in1=sg[:, ro : ro + 128].unsqueeze(1).to_broadcast([P, 4, 128]),
+                    op=ALU.mult,
+                )
+                nc.vector.tensor_tensor(
+                    out=xf[:, 512:768].rearrange("p (w m) -> p w m", w=2),
+                    in0=xf[:, 512:768].rearrange("p (w m) -> p w m", w=2),
+                    in1=sg[:, ro + 128 : ro + 256].unsqueeze(1).to_broadcast([P, 2, 128]),
+                    op=ALU.mult,
+                )
+                for eb in range(2):
+                    nc.scalar.copy(
+                        out=xf[:, 768 + 128 * eb : 896 + 128 * eb].rearrange(
+                            "p (ra ea rb) -> p ra ea rb", ra=8, ea=2
+                        ),
+                        in_=xf[:, 256:512]
+                        .rearrange("p (ea rb eb ra) -> p eb ra ea rb", ea=2, rb=8, eb=2)[:, eb],
+                    )
+                xt = ps_t.tile([P, 8, P], BF16, tag="tp")
+                for c, u, z in ((0, 0, 0), (0, 1, 1), (1, 0, 3), (1, 1, 2)):
+                    for e in range(2):
+                        lo = z * 256 + e * 128
+                        nc.tensor.transpose(
+                            out=xt[:, 4 * c + 2 * u + e, :], in_=xf[:, lo : lo + 128], identity=ident_bf[:]
+                        )
+                nc.scalar.copy(
+                    out=grp[:, kk * K : (kk + 1) * K].rearrange("p (c n t) -> p c n t", c=2, t=4),
+                    in_=xt[:].rearrange("p (c t) n -> p c n t", c=2),
+                )
+            x_cod = cpool.tile([P, 512], U32, align_bytes=64)
+            x_scl = cpool.tile([P, 512], U8, align_bytes=64)
+            nc.vector.quantize_mx(out=x_cod[:].bitcast(FP8X4), scales=x_scl[:], in_=grp[:])
+            o_sb = opool.tile([P, 2, C], F32)
+            for kk in range(2):
+                for h in range(2):
+                    acc = ps_o.tile([P, 512], F32)
+                    for c in range(2):
+                        lo = c * C + h * 512
+                        xo = kk * 256 + c * P
+                        nc.tensor.matmul_mx(
+                            out=acc[:],
+                            lhsT=x_cod[:, xo : xo + P].bitcast(FP8X4),
+                            lhsT_scale=x_scl[:, xo : xo + P],
+                            rhs=w_cod[:, lo : lo + 512].bitcast(FP8X4),
+                            rhs_scale=w_scl[:, lo : lo + 512],
+                            start=(c == 0),
+                            stop=(c == 1),
+                        )
+                    nc.vector.tensor_tensor(
+                        out=o_sb[:, kk, h * 512 : (h + 1) * 512],
+                        in0=acc[:],
+                        in1=bias_bf[:, h * 512 : (h + 1) * 512],
+                        op=ALU.add,
+                    )
+            nc.sync.dma_start(out=out_v[:, 2 * kp : 2 * kp + 2, :], in_=o_sb[:])

@@ -24,12 +24,13 @@ FLOPS = 2 * B * K * C
 def tile_bcnnresnet_t_kernel(tc, feat, W, b, out):
     nc = tc.nc
     with ExitStack() as ctx:
+        ctx.enter_context(tc.manual_schedule())
         keep = ctx.enter_context(tc.tile_pool(name="keep", bufs=1))
-        qpool = ctx.enter_context(tc.tile_pool(name="qpool", bufs=4))
-        xpool = ctx.enter_context(tc.tile_pool(name="xpool", bufs=6))
+        qpool = ctx.enter_context(tc.tile_pool(name="qpool", bufs=3))
+        xpool = ctx.enter_context(tc.tile_pool(name="xpool", bufs=5))
         gpool = ctx.enter_context(tc.tile_pool(name="gpool", bufs=3))
         cpool = ctx.enter_context(tc.tile_pool(name="cpool", bufs=3))
-        opool = ctx.enter_context(tc.tile_pool(name="opool", bufs=4))
+        opool = ctx.enter_context(tc.tile_pool(name="opool", bufs=6))
         ps_t = ctx.enter_context(tc.psum_pool(name="ps_t", bufs=2))
         ps_s = ctx.enter_context(tc.psum_pool(name="ps_s", bufs=2))
         ps_o = ctx.enter_context(tc.psum_pool(name="ps_o", bufs=4))
@@ -64,28 +65,28 @@ def tile_bcnnresnet_t_kernel(tc, feat, W, b, out):
 
         a_nat = keep.tile([P, NT * D], BF16)
         nc.scalar.activation(out=a_nat[:], in_=f_sb[:], func=ACTF.Abs)
-        s_nat = keep.tile([P, NT * D], BF16)
-        nc.scalar.activation(out=s_nat[:], in_=f_sb[:], func=ACTF.Sign)
         a_per = keep.tile([P, NT * D], BF16)
         nc.scalar.activation(
             out=a_per[:].rearrange("p (m e r) -> p m e r", e=2, r=8),
             in_=f_sb[:].rearrange("p (m r e) -> p m e r", e=2, r=8),
             func=ACTF.Abs,
         )
+        s_nat = keep.tile([P, NT * D], BF16)
+        nc.scalar.activation(out=s_nat[:], in_=f_sb[:], func=ACTF.Sign)
         nz = keep.tile([P, NT * D], BF16)
-        nc.scalar.activation(out=nz[:], in_=s_nat[:], func=ACTF.Abs)
-        sum_a = keep.tile([P, NT], F32)
-        nc.vector.tensor_reduce(
-            out=sum_a[:], in_=a_nat[:].rearrange("p (t d) -> p t d", d=D), axis=AX.X, op=ALU.add
-        )
+        nc.vector.tensor_single_scalar(out=nz[:], in_=f_sb[:], scalar=0.0, op=ALU.not_equal)
         cnt = keep.tile([P, NT], F32)
         nc.vector.tensor_reduce(
             out=cnt[:], in_=nz[:].rearrange("p (t d) -> p t d", d=D), axis=AX.X, op=ALU.add
         )
-        sq_a = keep.tile([P, NT], F32)
-        nc.vector.tensor_tensor(out=sq_a[:], in0=sum_a[:], in1=sum_a[:], op=ALU.mult)
         sq_c = keep.tile([P, NT], F32)
         nc.vector.tensor_tensor(out=sq_c[:], in0=cnt[:], in1=cnt[:], op=ALU.mult)
+        sum_a = keep.tile([P, NT], F32)
+        nc.vector.tensor_reduce(
+            out=sum_a[:], in_=a_nat[:].rearrange("p (t d) -> p t d", d=D), axis=AX.X, op=ALU.add
+        )
+        sq_a = keep.tile([P, NT], F32)
+        nc.vector.tensor_tensor(out=sq_a[:], in0=sum_a[:], in1=sum_a[:], op=ALU.mult)
         n2 = keep.tile([P, NT], F32)
         nc.vector.scalar_tensor_tensor(
             out=n2[:], in0=sq_c[:], scalar=EPS_SQRT, in1=sq_a[:], op0=ALU.mult, op1=ALU.add
@@ -109,7 +110,8 @@ def tile_bcnnresnet_t_kernel(tc, feat, W, b, out):
         raw_w = w_raw[:].bitcast(F32)
         ord_w = w_ord[:].bitcast(F32)
         grp_w = w_grp[:].bitcast(F32).rearrange("p (c n u) -> p c n u", c=2, u=2)
-        for ct in range(8):
+
+        def w_stage(ct):
             for c in range(2):
                 lo = ct * 512 + c * 256
                 nc.scalar.copy(
@@ -135,7 +137,9 @@ def tile_bcnnresnet_t_kernel(tc, feat, W, b, out):
                     )
 
         out_v = out.rearrange("(p t) c -> p t c", t=NT)
-        for kp in range(NT // 2):
+        t_q, t_x, t_sg, t_xt, t_g, t_c, t_acc = {}, {}, {}, {}, {}, {}, {}
+
+        def st_sign(kp):
             g, hh = kp // 2, kp % 2
             sg = ps_s.tile([P, 1024], BF16)
             nc.tensor.matmul(
@@ -144,111 +148,151 @@ def tile_bcnnresnet_t_kernel(tc, feat, W, b, out):
             nc.tensor.matmul(
                 out=sg[:, 512:576], lhsT=s_t[:, g, :], rhs=sel_per[:, hh * 64 : (hh + 1) * 64], start=True, stop=True
             )
-            grp = gpool.tile([P, 2 * K], BF16, align_bytes=64)
-            for kk in range(2):
-                k = 2 * kp + kk
-                fo = k * D
-                q32 = qpool.tile([P, 768], F32)
-                nc.gpsimd.tensor_tensor(
-                    out=q32[:, 0:512].rearrange("p (w q r) -> p w q r", w=4, r=8),
-                    in0=a_nat[:, fo : fo + 16].unsqueeze(1).unsqueeze(3).to_broadcast([P, 4, 16, 8]),
-                    in1=a_per[:, fo : fo + 32]
-                    .rearrange("p (w r) -> p w r", r=8)
-                    .unsqueeze(2)
-                    .to_broadcast([P, 4, 16, 8]),
-                    op=ALU.mult,
-                )
-                nc.gpsimd.tensor_tensor(
-                    out=q32[:, 512:768].rearrange("p (w q r) -> p w q r", w=2, r=8),
-                    in0=a_nat[:, fo + 16 : fo + 32].unsqueeze(1).unsqueeze(3).to_broadcast([P, 2, 16, 8]),
-                    in1=a_per[:, fo + 16 : fo + 32]
-                    .rearrange("p (w r) -> p w r", r=8)
-                    .unsqueeze(2)
-                    .to_broadcast([P, 2, 16, 8]),
-                    op=ALU.mult,
-                )
-                xf = xpool.tile([P, K], BF16)
-                nc.scalar.activation(
-                    out=xf[:, 0:768],
-                    in_=q32[:],
-                    func=ACTF.Sqrt,
-                    bias=erho[:, k : k + 1],
-                    scale=rho[:, k : k + 1],
-                )
-                so = 512 + kk * 32
-                ro = kk * 256
-                nc.vector.tensor_tensor(
-                    out=xf[:, 0:512].rearrange("p (w q r) -> p w q r", w=4, r=8),
-                    in0=xf[:, 0:512].rearrange("p (w q r) -> p w q r", w=4, r=8),
-                    in1=sg[:, so : so + 32]
-                    .rearrange("p (w r) -> p w r", r=8)
-                    .unsqueeze(2)
-                    .to_broadcast([P, 4, 16, 8]),
-                    op=ALU.mult,
-                )
-                nc.vector.tensor_tensor(
-                    out=xf[:, 512:768].rearrange("p (w q r) -> p w q r", w=2, r=8),
-                    in0=xf[:, 512:768].rearrange("p (w q r) -> p w q r", w=2, r=8),
-                    in1=sg[:, so + 16 : so + 32]
-                    .rearrange("p (w r) -> p w r", r=8)
-                    .unsqueeze(2)
-                    .to_broadcast([P, 2, 16, 8]),
-                    op=ALU.mult,
-                )
-                nc.vector.tensor_tensor(
-                    out=xf[:, 0:512].rearrange("p (w m) -> p w m", w=4),
-                    in0=xf[:, 0:512].rearrange("p (w m) -> p w m", w=4),
-                    in1=sg[:, ro : ro + 128].unsqueeze(1).to_broadcast([P, 4, 128]),
-                    op=ALU.mult,
-                )
-                nc.vector.tensor_tensor(
-                    out=xf[:, 512:768].rearrange("p (w m) -> p w m", w=2),
-                    in0=xf[:, 512:768].rearrange("p (w m) -> p w m", w=2),
-                    in1=sg[:, ro + 128 : ro + 256].unsqueeze(1).to_broadcast([P, 2, 128]),
-                    op=ALU.mult,
-                )
-                for eb in range(2):
-                    nc.scalar.copy(
-                        out=xf[:, 768 + 128 * eb : 896 + 128 * eb].rearrange(
-                            "p (ra ea rb) -> p ra ea rb", ra=8, ea=2
-                        ),
-                        in_=xf[:, 256:512]
-                        .rearrange("p (ea rb eb ra) -> p eb ra ea rb", ea=2, rb=8, eb=2)[:, eb],
-                    )
-                xt = ps_t.tile([P, 8, P], BF16, tag="tp")
-                for c, u, z in ((0, 0, 0), (0, 1, 1), (1, 0, 3), (1, 1, 2)):
-                    for e in range(2):
-                        lo = z * 256 + e * 128
-                        nc.tensor.transpose(
-                            out=xt[:, 4 * c + 2 * u + e, :], in_=xf[:, lo : lo + 128], identity=ident_bf[:]
-                        )
+            t_sg[kp] = sg
+
+        def st_prod(k):
+            fo = k * D
+            q32 = qpool.tile([P, 768], F32)
+            nc.gpsimd.tensor_tensor(
+                out=q32[:, 0:512].rearrange("p (w q r) -> p w q r", w=4, r=8),
+                in0=a_nat[:, fo : fo + 16].unsqueeze(1).unsqueeze(3).to_broadcast([P, 4, 16, 8]),
+                in1=a_per[:, fo : fo + 32].rearrange("p (w r) -> p w r", r=8).unsqueeze(2).to_broadcast([P, 4, 16, 8]),
+                op=ALU.mult,
+            )
+            nc.gpsimd.tensor_tensor(
+                out=q32[:, 512:768].rearrange("p (w q r) -> p w q r", w=2, r=8),
+                in0=a_nat[:, fo + 16 : fo + 32].unsqueeze(1).unsqueeze(3).to_broadcast([P, 2, 16, 8]),
+                in1=a_per[:, fo + 16 : fo + 32]
+                .rearrange("p (w r) -> p w r", r=8)
+                .unsqueeze(2)
+                .to_broadcast([P, 2, 16, 8]),
+                op=ALU.mult,
+            )
+            t_q[k] = q32
+
+        def st_sqrt(k):
+            xf = xpool.tile([P, K], BF16)
+            nc.scalar.activation(
+                out=xf[:, 0:768], in_=t_q[k][:], func=ACTF.Sqrt, bias=erho[:, k : k + 1], scale=rho[:, k : k + 1]
+            )
+            t_x[k] = xf
+
+        def st_signs(k):
+            xf, sg = t_x[k], t_sg[k // 2]
+            so = 512 + (k % 2) * 32
+            ro = (k % 2) * 256
+            nc.vector.tensor_tensor(
+                out=xf[:, 0:512].rearrange("p (w q r) -> p w q r", w=4, r=8),
+                in0=xf[:, 0:512].rearrange("p (w q r) -> p w q r", w=4, r=8),
+                in1=sg[:, so : so + 32].rearrange("p (w r) -> p w r", r=8).unsqueeze(2).to_broadcast([P, 4, 16, 8]),
+                op=ALU.mult,
+            )
+            nc.vector.tensor_tensor(
+                out=xf[:, 0:512].rearrange("p (w m) -> p w m", w=4),
+                in0=xf[:, 0:512].rearrange("p (w m) -> p w m", w=4),
+                in1=sg[:, ro : ro + 128].unsqueeze(1).to_broadcast([P, 4, 128]),
+                op=ALU.mult,
+            )
+            nc.vector.tensor_tensor(
+                out=xf[:, 512:768].rearrange("p (w q r) -> p w q r", w=2, r=8),
+                in0=xf[:, 512:768].rearrange("p (w q r) -> p w q r", w=2, r=8),
+                in1=sg[:, so + 16 : so + 32]
+                .rearrange("p (w r) -> p w r", r=8)
+                .unsqueeze(2)
+                .to_broadcast([P, 2, 16, 8]),
+                op=ALU.mult,
+            )
+            nc.vector.tensor_tensor(
+                out=xf[:, 512:768].rearrange("p (w m) -> p w m", w=2),
+                in0=xf[:, 512:768].rearrange("p (w m) -> p w m", w=2),
+                in1=sg[:, ro + 128 : ro + 256].unsqueeze(1).to_broadcast([P, 2, 128]),
+                op=ALU.mult,
+            )
+
+        def st_mirror(k):
+            xf = t_x[k]
+            for eb in range(2):
                 nc.scalar.copy(
-                    out=grp[:, kk * K : (kk + 1) * K].rearrange("p (c n t) -> p c n t", c=2, t=4),
-                    in_=xt[:].rearrange("p (c t) n -> p c n t", c=2),
+                    out=xf[:, 768 + 128 * eb : 896 + 128 * eb].rearrange("p (ra ea rb) -> p ra ea rb", ra=8, ea=2),
+                    in_=xf[:, 256:512].rearrange("p (ea rb eb ra) -> p eb ra ea rb", ea=2, rb=8, eb=2)[:, eb],
                 )
-            x_cod = cpool.tile([P, 512], U32, align_bytes=64)
-            x_scl = cpool.tile([P, 512], U8, align_bytes=64)
-            nc.vector.quantize_mx(out=x_cod[:].bitcast(FP8X4), scales=x_scl[:], in_=grp[:])
-            o_sb = opool.tile([P, 2, C], F32)
-            for kk in range(2):
-                for h in range(2):
-                    acc = ps_o.tile([P, 512], F32)
-                    for c in range(2):
-                        lo = c * C + h * 512
-                        xo = kk * 256 + c * P
-                        nc.tensor.matmul_mx(
-                            out=acc[:],
-                            lhsT=x_cod[:, xo : xo + P].bitcast(FP8X4),
-                            lhsT_scale=x_scl[:, xo : xo + P],
-                            rhs=w_cod[:, lo : lo + 512].bitcast(FP8X4),
-                            rhs_scale=w_scl[:, lo : lo + 512],
-                            start=(c == 0),
-                            stop=(c == 1),
-                        )
-                    nc.vector.tensor_tensor(
-                        out=o_sb[:, kk, h * 512 : (h + 1) * 512],
-                        in0=acc[:],
-                        in1=bias_bf[:, h * 512 : (h + 1) * 512],
-                        op=ALU.add,
+
+        def st_transpose(k):
+            xf = t_x[k]
+            xt = ps_t.tile([P, 8, P], BF16, tag="tp")
+            for c, u, z in ((0, 0, 0), (0, 1, 1), (1, 0, 3), (1, 1, 2)):
+                for e in range(2):
+                    lo = z * 256 + e * 128
+                    nc.tensor.transpose(
+                        out=xt[:, 4 * c + 2 * u + e, :], in_=xf[:, lo : lo + 128], identity=ident_bf[:]
                     )
-            nc.sync.dma_start(out=out_v[:, 2 * kp : 2 * kp + 2, :], in_=o_sb[:])
+            t_xt[k] = xt
+
+        def st_group(k):
+            grp = gpool.tile([P, K], BF16, align_bytes=64)
+            nc.scalar.copy(
+                out=grp[:].rearrange("p (c n t) -> p c n t", c=2, t=4),
+                in_=t_xt[k][:].rearrange("p (c t) n -> p c n t", c=2),
+            )
+            t_g[k] = grp
+
+        def st_quant(k):
+            x_cod = cpool.tile([P, 256], U32, align_bytes=64)
+            x_scl = cpool.tile([P, 256], U8, align_bytes=64)
+            nc.vector.quantize_mx(out=x_cod[:].bitcast(FP8X4), scales=x_scl[:], in_=t_g[k][:])
+            t_c[k] = (x_cod, x_scl)
+
+        def st_mx(k):
+            x_cod, x_scl = t_c[k]
+            for h in range(2):
+                acc = ps_o.tile([P, 512], F32)
+                for c in range(2):
+                    lo = c * C + h * 512
+                    nc.tensor.matmul_mx(
+                        out=acc[:],
+                        lhsT=x_cod[:, c * P : (c + 1) * P].bitcast(FP8X4),
+                        lhsT_scale=x_scl[:, c * P : (c + 1) * P],
+                        rhs=w_cod[:, lo : lo + 512].bitcast(FP8X4),
+                        rhs_scale=w_scl[:, lo : lo + 512],
+                        start=(c == 0),
+                        stop=(c == 1),
+                    )
+                t_acc[(k, h)] = acc
+
+        def st_out(k):
+            o_sb = opool.tile([P, C], F32)
+            for h in range(2):
+                nc.vector.tensor_tensor(
+                    out=o_sb[:, h * 512 : (h + 1) * 512],
+                    in0=t_acc[(k, h)][:],
+                    in1=bias_bf[:, h * 512 : (h + 1) * 512],
+                    op=ALU.add,
+                )
+            nc.sync.dma_start(out=out_v[:, k, :], in_=o_sb[:])
+
+        def on(k):
+            return 0 <= k < NT
+
+        st_sign(0)
+        for s in range(NT + 4):
+            if on(s):
+                st_prod(s)
+            if on(s - 1):
+                st_sqrt(s - 1)
+            if on(s - 2):
+                st_signs(s - 2)
+            if on(s - 3):
+                st_transpose(s - 3)
+                st_group(s - 3)
+            if on(s - 2):
+                st_mirror(s - 2)
+            if on(s - 4):
+                st_mx(s - 4)
+                st_out(s - 4)
+            if on(s - 3):
+                st_quant(s - 3)
+            if s % 2 == 1 and on(s + 1):
+                st_sign((s + 1) // 2)
+            if s < 4:
+                w_stage(2 * s)
+                w_stage(2 * s + 1)

@@ -111,13 +111,15 @@ def tile_bcnnresnet_t_kernel(tc, feat, W, b, out):
         ord_w = w_ord[:].bitcast(F32)
         grp_w = w_grp[:].bitcast(F32).rearrange("p (c n u) -> p c n u", c=2, u=2)
 
-        def w_stage(ct):
+        for ct in range(8):
             for c in range(2):
                 lo = ct * 512 + c * 256
-                nc.scalar.copy(
+                nc.vector.tensor_copy(
                     out=ord_w[:, lo : lo + 256].rearrange("p (u q r) -> p u q r", u=2, r=8),
                     in_=raw_w[:, lo : lo + 256].rearrange("p (q u r) -> p u q r", u=2, r=8),
                 )
+
+        def w_stage(ct):
             wt = ps_t.tile([P, 4, P], F32, tag="tp")
             for s in range(4):
                 lo = ct * 512 + s * 128
@@ -137,7 +139,7 @@ def tile_bcnnresnet_t_kernel(tc, feat, W, b, out):
                     )
 
         out_v = out.rearrange("(p t) c -> p t c", t=NT)
-        t_q, t_x, t_sg, t_xt, t_g, t_c, t_acc = {}, {}, {}, {}, {}, {}, {}
+        t_q, t_x, t_sg, t_xt, t_g, t_c, t_acc, t_o = {}, {}, {}, {}, {}, {}, {}, {}
 
         def st_sign(kp):
             g, hh = kp // 2, kp % 2
@@ -177,20 +179,13 @@ def tile_bcnnresnet_t_kernel(tc, feat, W, b, out):
             )
             t_x[k] = xf
 
-        def st_signs(k):
+        def st_sign_col(k):
             xf, sg = t_x[k], t_sg[k // 2]
             so = 512 + (k % 2) * 32
-            ro = (k % 2) * 256
             nc.vector.tensor_tensor(
                 out=xf[:, 0:512].rearrange("p (w q r) -> p w q r", w=4, r=8),
                 in0=xf[:, 0:512].rearrange("p (w q r) -> p w q r", w=4, r=8),
                 in1=sg[:, so : so + 32].rearrange("p (w r) -> p w r", r=8).unsqueeze(2).to_broadcast([P, 4, 16, 8]),
-                op=ALU.mult,
-            )
-            nc.vector.tensor_tensor(
-                out=xf[:, 0:512].rearrange("p (w m) -> p w m", w=4),
-                in0=xf[:, 0:512].rearrange("p (w m) -> p w m", w=4),
-                in1=sg[:, ro : ro + 128].unsqueeze(1).to_broadcast([P, 4, 128]),
                 op=ALU.mult,
             )
             nc.vector.tensor_tensor(
@@ -200,6 +195,16 @@ def tile_bcnnresnet_t_kernel(tc, feat, W, b, out):
                 .rearrange("p (w r) -> p w r", r=8)
                 .unsqueeze(2)
                 .to_broadcast([P, 2, 16, 8]),
+                op=ALU.mult,
+            )
+
+        def st_sign_row(k):
+            xf, sg = t_x[k], t_sg[k // 2]
+            ro = (k % 2) * 256
+            nc.vector.tensor_tensor(
+                out=xf[:, 0:512].rearrange("p (w m) -> p w m", w=4),
+                in0=xf[:, 0:512].rearrange("p (w m) -> p w m", w=4),
+                in1=sg[:, ro : ro + 128].unsqueeze(1).to_broadcast([P, 4, 128]),
                 op=ALU.mult,
             )
             nc.vector.tensor_tensor(
@@ -259,40 +264,48 @@ def tile_bcnnresnet_t_kernel(tc, feat, W, b, out):
                     )
                 t_acc[(k, h)] = acc
 
-        def st_out(k):
-            o_sb = opool.tile([P, C], F32)
-            for h in range(2):
-                nc.vector.tensor_tensor(
-                    out=o_sb[:, h * 512 : (h + 1) * 512],
-                    in0=t_acc[(k, h)][:],
-                    in1=bias_bf[:, h * 512 : (h + 1) * 512],
-                    op=ALU.add,
-                )
-            nc.sync.dma_start(out=out_v[:, k, :], in_=o_sb[:])
+        def st_out(k, h):
+            if h == 0:
+                o_new = opool.tile([P, C], F32, name="o_sb")
+                t_o[k] = o_new
+            o_sb = t_o[k]
+            nc.vector.tensor_tensor(
+                out=o_sb[:, h * 512 : (h + 1) * 512],
+                in0=t_acc[(k, h)][:],
+                in1=bias_bf[:, h * 512 : (h + 1) * 512],
+                op=ALU.add,
+            )
+            if h == 1:
+                nc.sync.dma_start(out=out_v[:, k, :], in_=o_sb[:])
 
         def on(k):
             return 0 <= k < NT
 
         st_sign(0)
-        for s in range(NT + 4):
+        for s in range(NT + 6):
             if on(s):
                 st_prod(s)
             if on(s - 1):
                 st_sqrt(s - 1)
-            if on(s - 2):
-                st_signs(s - 2)
             if on(s - 3):
                 st_transpose(s - 3)
-                st_group(s - 3)
+            if on(s - 2):
+                st_sign_col(s - 2)
+            if on(s - 6):
+                st_out(s - 6, 0)
+            if on(s - 2):
+                st_sign_row(s - 2)
+            if on(s - 6):
+                st_out(s - 6, 1)
+            if on(s - 4):
+                st_quant(s - 4)
             if on(s - 2):
                 st_mirror(s - 2)
-            if on(s - 4):
-                st_mx(s - 4)
-                st_out(s - 4)
             if on(s - 3):
-                st_quant(s - 3)
+                st_group(s - 3)
+            if on(s - 5):
+                st_mx(s - 5)
             if s % 2 == 1 and on(s + 1):
                 st_sign((s + 1) // 2)
-            if s < 4:
-                w_stage(2 * s)
-                w_stage(2 * s + 1)
+            for ct in range(3 * s, min(3 * s + 3, 8)):
+                w_stage(ct)

@@ -19,6 +19,7 @@ NT = B // P
 EPS_SQRT = 1e-10
 EPS_NORM = 1e-12
 FLOPS = 2 * B * K * C
+HEAD = 8
 
 
 def tile_bcnnresnet_t_kernel(tc, feat, W, b, out):
@@ -52,56 +53,120 @@ def tile_bcnnresnet_t_kernel(tc, feat, W, b, out):
         ident_f = keep.tile([P, P], F32)
         make_identity(nc, ident_f[:])
 
-        sel_rep = keep.tile([P, P * 8], BF16)
-        nc.vector.tensor_copy(
-            out=sel_rep[:].rearrange("p (m r) -> p m r", r=8),
-            in_=ident_bf[:].unsqueeze(2).to_broadcast([P, P, 8]),
-        )
         sel_per = keep.tile([P, P], BF16)
-        nc.vector.tensor_copy(
-            out=sel_per[:].rearrange("p (m e r) -> p m e r", e=2, r=8),
-            in_=ident_bf[:].rearrange("p (m r e) -> p m e r", e=2, r=8),
-        )
+        sel_col = keep.tile([P, 4 * 48], BF16)
+        sel_row = keep.tile([P, 4 * 384], BF16)
+
+        def sel_small():
+            nc.vector.tensor_copy(
+                out=sel_per[:].rearrange("p (m e r) -> p m e r", e=2, r=8),
+                in_=ident_bf[:].rearrange("p (m r e) -> p m e r", e=2, r=8),
+            )
+            nc.vector.tensor_copy(
+                out=sel_col[:].rearrange("p (a w) -> p a w", a=4)[:, :, 0:32],
+                in_=sel_per[:].rearrange("p (a w) -> p a w", a=4),
+            )
+            nc.vector.tensor_copy(
+                out=sel_col[:].rearrange("p (a w) -> p a w", a=4)[:, :, 32:48],
+                in_=sel_per[:].rearrange("p (a w) -> p a w", a=4)[:, :, 16:32],
+            )
+
+        def sel_big(a, part):
+            lo = a * 384
+            if part == 0:
+                nc.vector.tensor_copy(
+                    out=sel_row[:, lo : lo + 256].rearrange("p (z q r) -> p z q r", z=2, r=8),
+                    in_=ident_bf[:, 32 * a : 32 * a + 16].unsqueeze(1).unsqueeze(3).to_broadcast([P, 2, 16, 8]),
+                )
+            else:
+                nc.vector.tensor_copy(
+                    out=sel_row[:, lo + 256 : lo + 384].rearrange("p (q r) -> p q r", r=8),
+                    in_=ident_bf[:, 32 * a + 16 : 32 * a + 32].unsqueeze(2).to_broadcast([P, 16, 8]),
+                )
 
         a_nat = keep.tile([P, NT * D], BF16)
-        nc.scalar.activation(out=a_nat[:], in_=f_sb[:], func=ACTF.Abs)
         a_per = keep.tile([P, NT * D], BF16)
-        nc.scalar.activation(
-            out=a_per[:].rearrange("p (m e r) -> p m e r", e=2, r=8),
-            in_=f_sb[:].rearrange("p (m r e) -> p m e r", e=2, r=8),
-            func=ACTF.Abs,
-        )
         s_nat = keep.tile([P, NT * D], BF16)
-        nc.scalar.activation(out=s_nat[:], in_=f_sb[:], func=ACTF.Sign)
         nz = keep.tile([P, NT * D], BF16)
-        nc.vector.tensor_single_scalar(out=nz[:], in_=f_sb[:], scalar=0.0, op=ALU.not_equal)
         cnt = keep.tile([P, NT], F32)
-        nc.vector.tensor_reduce(
-            out=cnt[:], in_=nz[:].rearrange("p (t d) -> p t d", d=D), axis=AX.X, op=ALU.add
-        )
         sq_c = keep.tile([P, NT], F32)
-        nc.vector.tensor_tensor(out=sq_c[:], in0=cnt[:], in1=cnt[:], op=ALU.mult)
         sum_a = keep.tile([P, NT], F32)
-        nc.vector.tensor_reduce(
-            out=sum_a[:], in_=a_nat[:].rearrange("p (t d) -> p t d", d=D), axis=AX.X, op=ALU.add
-        )
         sq_a = keep.tile([P, NT], F32)
-        nc.vector.tensor_tensor(out=sq_a[:], in0=sum_a[:], in1=sum_a[:], op=ALU.mult)
         n2 = keep.tile([P, NT], F32)
-        nc.vector.scalar_tensor_tensor(
-            out=n2[:], in0=sq_c[:], scalar=EPS_SQRT, in1=sq_a[:], op0=ALU.mult, op1=ALU.add
-        )
         n2c = keep.tile([P, NT], F32)
-        nc.vector.tensor_scalar_max(out=n2c[:], in0=n2[:], scalar1=EPS_NORM * EPS_NORM)
         rho = keep.tile([P, NT], F32)
-        nc.vector.reciprocal(out=rho[:], in_=n2c[:])
         erho = keep.tile([P, NT], F32)
-        nc.vector.tensor_scalar_mul(out=erho[:], in0=rho[:], scalar1=EPS_SQRT)
-        st_ps = ps_t.tile([P, 8, P], BF16, tag="tp")
-        for g in range(8):
-            nc.tensor.transpose(out=st_ps[:, g, :], in_=s_nat[:, g * P : (g + 1) * P], identity=ident_bf[:])
         s_t = keep.tile([P, 8, P], BF16)
-        nc.scalar.copy(out=s_t[:], in_=st_ps[:])
+
+        def scalar_prep(t0, t1):
+            lo, hi = t0 * D, t1 * D
+            nc.scalar.activation(out=a_nat[:, lo:hi], in_=f_sb[:, lo:hi], func=ACTF.Abs)
+            nc.scalar.activation(
+                out=a_per[:, lo:hi].rearrange("p (m e r) -> p m e r", e=2, r=8),
+                in_=f_sb[:, lo:hi].rearrange("p (m r e) -> p m e r", e=2, r=8),
+                func=ACTF.Abs,
+            )
+            nc.scalar.activation(out=s_nat[:, lo:hi], in_=f_sb[:, lo:hi], func=ACTF.Sign)
+
+        def vector_prep(t0, t1):
+            lo, hi = t0 * D, t1 * D
+            ts = slice(t0, t1)
+            return [
+                lambda: nc.vector.tensor_single_scalar(
+                    out=nz[:, lo:hi], in_=f_sb[:, lo:hi], scalar=0.0, op=ALU.not_equal
+                ),
+                lambda: nc.vector.tensor_reduce(
+                    out=cnt[:, ts], in_=nz[:, lo:hi].rearrange("p (t d) -> p t d", d=D), axis=AX.X, op=ALU.add
+                ),
+                lambda: nc.vector.tensor_reduce(
+                    out=sum_a[:, ts], in_=a_nat[:, lo:hi].rearrange("p (t d) -> p t d", d=D), axis=AX.X, op=ALU.add
+                ),
+                lambda: nc.vector.tensor_tensor(out=sq_c[:, ts], in0=cnt[:, ts], in1=cnt[:, ts], op=ALU.mult),
+                lambda: nc.vector.tensor_tensor(out=sq_a[:, ts], in0=sum_a[:, ts], in1=sum_a[:, ts], op=ALU.mult),
+                lambda: nc.vector.scalar_tensor_tensor(
+                    out=n2[:, ts], in0=sq_c[:, ts], scalar=EPS_SQRT, in1=sq_a[:, ts], op0=ALU.mult, op1=ALU.add
+                ),
+                lambda: nc.vector.tensor_scalar_max(out=n2c[:, ts], in0=n2[:, ts], scalar1=EPS_NORM * EPS_NORM),
+                lambda: nc.vector.reciprocal(out=rho[:, ts], in_=n2c[:, ts]),
+                lambda: nc.vector.tensor_scalar_mul(out=erho[:, ts], in0=rho[:, ts], scalar1=EPS_SQRT),
+            ]
+
+        def sign_rows(g0, g1):
+            st_ps = ps_t.tile([P, 8, P], BF16, tag="tp")
+            for g in range(g0, g1):
+                nc.tensor.transpose(
+                    out=st_ps[:, g, :], in_=s_nat[:, g * P : (g + 1) * P], identity=ident_bf[:]
+                )
+            nc.scalar.copy(out=s_t[:, g0:g1, :], in_=st_ps[:, g0:g1, :])
+
+        sel_small()
+        sel_big(0, 0)
+        sel_big(0, 1)
+        scalar_prep(0, HEAD)
+        scalar_prep(HEAD, NT)
+        first, rest = vector_prep(0, HEAD), vector_prep(HEAD, NT)
+        fill = [(a, part) for a in range(1, 4) for part in range(2)]
+        first[0]()
+        rest[0]()
+        first[1]()
+        first[2]()
+        sel_big(*fill[0])
+        first[3]()
+        first[4]()
+        sel_big(*fill[1])
+        sel_big(*fill[2])
+        first[5]()
+        rest[1]()
+        first[6]()
+        rest[2]()
+        first[7]()
+        sel_big(*fill[3])
+        sel_big(*fill[4])
+        sel_big(*fill[5])
+        first[8]()
+        for step in rest[3:]:
+            step()
+        sign_rows(0, HEAD // 4)
 
         w_ord = keep.tile([P, 8 * K], BF16)
         w_grp = keep.tile([P, 2 * C * 4], BF16, align_bytes=64)
@@ -144,11 +209,17 @@ def tile_bcnnresnet_t_kernel(tc, feat, W, b, out):
         def st_sign(kp):
             g, hh = kp // 2, kp % 2
             sg = ps_s.tile([P, 1024], BF16)
+            for kk in range(2):
+                a = 2 * hh + kk
+                nc.tensor.matmul(
+                    out=sg[:, kk * 384 : (kk + 1) * 384],
+                    lhsT=s_t[:, g, :],
+                    rhs=sel_row[:, a * 384 : (a + 1) * 384],
+                    start=True,
+                    stop=True,
+                )
             nc.tensor.matmul(
-                out=sg[:, 0:512], lhsT=s_t[:, g, :], rhs=sel_rep[:, hh * 512 : (hh + 1) * 512], start=True, stop=True
-            )
-            nc.tensor.matmul(
-                out=sg[:, 512:576], lhsT=s_t[:, g, :], rhs=sel_per[:, hh * 64 : (hh + 1) * 64], start=True, stop=True
+                out=sg[:, 768:864], lhsT=s_t[:, g, :], rhs=sel_col[:, hh * 96 : (hh + 1) * 96], start=True, stop=True
             )
             t_sg[kp] = sg
 
@@ -181,43 +252,28 @@ def tile_bcnnresnet_t_kernel(tc, feat, W, b, out):
 
         def st_sign_col(k):
             xf, sg = t_x[k], t_sg[k // 2]
-            so = 512 + (k % 2) * 32
+            so = 768 + (k % 2) * 48
             nc.vector.tensor_tensor(
-                out=xf[:, 0:512].rearrange("p (w q r) -> p w q r", w=4, r=8),
-                in0=xf[:, 0:512].rearrange("p (w q r) -> p w q r", w=4, r=8),
-                in1=sg[:, so : so + 32].rearrange("p (w r) -> p w r", r=8).unsqueeze(2).to_broadcast([P, 4, 16, 8]),
-                op=ALU.mult,
-            )
-            nc.vector.tensor_tensor(
-                out=xf[:, 512:768].rearrange("p (w q r) -> p w q r", w=2, r=8),
-                in0=xf[:, 512:768].rearrange("p (w q r) -> p w q r", w=2, r=8),
-                in1=sg[:, so + 16 : so + 32]
-                .rearrange("p (w r) -> p w r", r=8)
-                .unsqueeze(2)
-                .to_broadcast([P, 2, 16, 8]),
+                out=xf[:, 0:768].rearrange("p (w q r) -> p w q r", w=6, r=8),
+                in0=xf[:, 0:768].rearrange("p (w q r) -> p w q r", w=6, r=8),
+                in1=sg[:, so : so + 48].rearrange("p (w r) -> p w r", r=8).unsqueeze(2).to_broadcast([P, 6, 16, 8]),
                 op=ALU.mult,
             )
 
         def st_sign_row(k):
             xf, sg = t_x[k], t_sg[k // 2]
-            ro = (k % 2) * 256
+            ro = (k % 2) * 384
             nc.vector.tensor_tensor(
-                out=xf[:, 0:512].rearrange("p (w m) -> p w m", w=4),
-                in0=xf[:, 0:512].rearrange("p (w m) -> p w m", w=4),
-                in1=sg[:, ro : ro + 128].unsqueeze(1).to_broadcast([P, 4, 128]),
-                op=ALU.mult,
-            )
-            nc.vector.tensor_tensor(
-                out=xf[:, 512:768].rearrange("p (w m) -> p w m", w=2),
-                in0=xf[:, 512:768].rearrange("p (w m) -> p w m", w=2),
-                in1=sg[:, ro + 128 : ro + 256].unsqueeze(1).to_broadcast([P, 2, 128]),
+                out=xf[:, 0:768].rearrange("p (z e m) -> p z e m", z=3, e=2),
+                in0=xf[:, 0:768].rearrange("p (z e m) -> p z e m", z=3, e=2),
+                in1=sg[:, ro : ro + 384].rearrange("p (z m) -> p z m", z=3).unsqueeze(2).to_broadcast([P, 3, 2, 128]),
                 op=ALU.mult,
             )
 
         def st_mirror(k):
             xf = t_x[k]
             for eb in range(2):
-                nc.scalar.copy(
+                nc.vector.tensor_copy(
                     out=xf[:, 768 + 128 * eb : 896 + 128 * eb].rearrange("p (ra ea rb) -> p ra ea rb", ra=8, ea=2),
                     in_=xf[:, 256:512].rearrange("p (ea rb eb ra) -> p eb ra ea rb", ea=2, rb=8, eb=2)[:, eb],
                 )
@@ -269,13 +325,11 @@ def tile_bcnnresnet_t_kernel(tc, feat, W, b, out):
                 o_new = opool.tile([P, C], F32, name="o_sb")
                 t_o[k] = o_new
             o_sb = t_o[k]
-            nc.vector.tensor_tensor(
-                out=o_sb[:, h * 512 : (h + 1) * 512],
-                in0=t_acc[(k, h)][:],
-                in1=bias_bf[:, h * 512 : (h + 1) * 512],
-                op=ALU.add,
-            )
-            if h == 1:
+            cols = slice(h * 512, (h + 1) * 512)
+            nc.vector.tensor_tensor(out=o_sb[:, cols], in0=t_acc[(k, h)][:], in1=bias_bf[:, cols], op=ALU.add)
+            if k == NT - 1:
+                nc.sync.dma_start(out=out_v[:, k, cols], in_=o_sb[:, cols])
+            elif h == 1:
                 nc.sync.dma_start(out=out_v[:, k, :], in_=o_sb[:])
 
         def on(k):
@@ -297,10 +351,10 @@ def tile_bcnnresnet_t_kernel(tc, feat, W, b, out):
                 st_sign_row(s - 2)
             if on(s - 6):
                 st_out(s - 6, 1)
-            if on(s - 4):
-                st_quant(s - 4)
             if on(s - 2):
                 st_mirror(s - 2)
+            if on(s - 4):
+                st_quant(s - 4)
             if on(s - 3):
                 st_group(s - 3)
             if on(s - 5):
@@ -309,3 +363,5 @@ def tile_bcnnresnet_t_kernel(tc, feat, W, b, out):
                 st_sign((s + 1) // 2)
             for ct in range(3 * s, min(3 * s + 3, 8)):
                 w_stage(ct)
+            if s == 1:
+                sign_rows(HEAD // 4, 8)

@@ -226,21 +226,17 @@ def tile_bcnnresnet_t_kernel(tc, feat, W, b, out):
         def st_prod(k):
             fo = k * D
             q32 = qpool.tile([P, 768], F32)
-            nc.gpsimd.tensor_tensor(
-                out=q32[:, 0:512].rearrange("p (w q r) -> p w q r", w=4, r=8),
-                in0=a_nat[:, fo : fo + 16].unsqueeze(1).unsqueeze(3).to_broadcast([P, 4, 16, 8]),
-                in1=a_per[:, fo : fo + 32].rearrange("p (w r) -> p w r", r=8).unsqueeze(2).to_broadcast([P, 4, 16, 8]),
-                op=ALU.mult,
-            )
-            nc.gpsimd.tensor_tensor(
-                out=q32[:, 512:768].rearrange("p (w q r) -> p w q r", w=2, r=8),
-                in0=a_nat[:, fo + 16 : fo + 32].unsqueeze(1).unsqueeze(3).to_broadcast([P, 2, 16, 8]),
-                in1=a_per[:, fo + 16 : fo + 32]
-                .rearrange("p (w r) -> p w r", r=8)
-                .unsqueeze(2)
-                .to_broadcast([P, 2, 16, 8]),
-                op=ALU.mult,
-            )
+            for z, c, u in ((0, 0, 0), (1, 0, 1), (2, 1, 1)):
+                ro, co = fo + 16 * c, fo + 16 * u
+                nc.gpsimd.tensor_tensor(
+                    out=q32[:, z * 256 : (z + 1) * 256].rearrange("p (w q r) -> p w q r", w=2, r=8),
+                    in0=a_nat[:, ro : ro + 16].unsqueeze(1).unsqueeze(3).to_broadcast([P, 2, 16, 8]),
+                    in1=a_per[:, co : co + 16]
+                    .rearrange("p (w r) -> p w r", r=8)
+                    .unsqueeze(2)
+                    .to_broadcast([P, 2, 16, 8]),
+                    op=ALU.mult,
+                )
             t_q[k] = q32
 
         def st_sqrt(k):
@@ -273,7 +269,7 @@ def tile_bcnnresnet_t_kernel(tc, feat, W, b, out):
         def st_mirror(k):
             xf = t_x[k]
             for eb in range(2):
-                nc.vector.tensor_copy(
+                nc.scalar.copy(
                     out=xf[:, 768 + 128 * eb : 896 + 128 * eb].rearrange("p (ra ea rb) -> p ra ea rb", ra=8, ea=2),
                     in_=xf[:, 256:512].rearrange("p (ea rb eb ra) -> p eb ra ea rb", ea=2, rb=8, eb=2)[:, eb],
                 )
@@ -351,10 +347,10 @@ def tile_bcnnresnet_t_kernel(tc, feat, W, b, out):
                 st_sign_row(s - 2)
             if on(s - 6):
                 st_out(s - 6, 1)
-            if on(s - 2):
-                st_mirror(s - 2)
             if on(s - 4):
                 st_quant(s - 4)
+            if on(s - 2):
+                st_mirror(s - 2)
             if on(s - 3):
                 st_group(s - 3)
             if on(s - 5):

@@ -27,7 +27,7 @@ def tile_bcnnresnet_t_kernel(tc, feat, W, b, out):
     with ExitStack() as ctx:
         ctx.enter_context(tc.manual_schedule())
         keep = ctx.enter_context(tc.tile_pool(name="keep", bufs=1))
-        qpool = ctx.enter_context(tc.tile_pool(name="qpool", bufs=3))
+        qpool = ctx.enter_context(tc.tile_pool(name="qpool", bufs=4))
         xpool = ctx.enter_context(tc.tile_pool(name="xpool", bufs=5))
         gpool = ctx.enter_context(tc.tile_pool(name="gpool", bufs=3))
         cpool = ctx.enter_context(tc.tile_pool(name="cpool", bufs=3))
@@ -84,8 +84,8 @@ def tile_bcnnresnet_t_kernel(tc, feat, W, b, out):
                     in_=ident_bf[:, 32 * a + 16 : 32 * a + 32].unsqueeze(2).to_broadcast([P, 16, 8]),
                 )
 
-        a_nat = keep.tile([P, NT * D], BF16)
-        a_per = keep.tile([P, NT * D], BF16)
+        a_nat = keep.tile([P, NT * D], F32)
+        a_per = keep.tile([P, NT * D], F32)
         s_nat = keep.tile([P, NT * D], BF16)
         nz = keep.tile([P, NT * D], BF16)
         cnt = keep.tile([P, NT], F32)
@@ -176,13 +176,14 @@ def tile_bcnnresnet_t_kernel(tc, feat, W, b, out):
         ord_w = w_ord[:].bitcast(F32)
         grp_w = w_grp[:].bitcast(F32).rearrange("p (c n u) -> p c n u", c=2, u=2)
 
-        for ct in range(8):
-            for c in range(2):
-                lo = ct * 512 + c * 256
-                nc.vector.tensor_copy(
-                    out=ord_w[:, lo : lo + 256].rearrange("p (u q r) -> p u q r", u=2, r=8),
-                    in_=raw_w[:, lo : lo + 256].rearrange("p (q u r) -> p u q r", u=2, r=8),
-                )
+        def w_reorder():
+            for ct in range(8):
+                for c in range(2):
+                    lo = ct * 512 + c * 256
+                    nc.vector.tensor_copy(
+                        out=ord_w[:, lo : lo + 256].rearrange("p (u q r) -> p u q r", u=2, r=8),
+                        in_=raw_w[:, lo : lo + 256].rearrange("p (q u r) -> p u q r", u=2, r=8),
+                    )
 
         def w_stage(ct):
             wt = ps_t.tile([P, 4, P], F32, tag="tp")
@@ -225,18 +226,22 @@ def tile_bcnnresnet_t_kernel(tc, feat, W, b, out):
 
         def st_prod(k):
             fo = k * D
+            nc.gpsimd.tensor_tensor(
+                out=t_q[k][:, 0:512].rearrange("p (w q r) -> p w q r", w=4, r=8),
+                in0=a_nat[:, fo : fo + 16].unsqueeze(1).unsqueeze(3).to_broadcast([P, 4, 16, 8]),
+                in1=a_per[:, fo : fo + 32].rearrange("p (w r) -> p w r", r=8).unsqueeze(2).to_broadcast([P, 4, 16, 8]),
+                op=ALU.mult,
+            )
+
+        def st_prod_v(k):
+            fo = k * D + 16
             q32 = qpool.tile([P, 768], F32)
-            for z, c, u in ((0, 0, 0), (1, 0, 1), (2, 1, 1)):
-                ro, co = fo + 16 * c, fo + 16 * u
-                nc.gpsimd.tensor_tensor(
-                    out=q32[:, z * 256 : (z + 1) * 256].rearrange("p (w q r) -> p w q r", w=2, r=8),
-                    in0=a_nat[:, ro : ro + 16].unsqueeze(1).unsqueeze(3).to_broadcast([P, 2, 16, 8]),
-                    in1=a_per[:, co : co + 16]
-                    .rearrange("p (w r) -> p w r", r=8)
-                    .unsqueeze(2)
-                    .to_broadcast([P, 2, 16, 8]),
-                    op=ALU.mult,
-                )
+            nc.vector.tensor_tensor(
+                out=q32[:, 512:768].rearrange("p (w q r) -> p w q r", w=2, r=8),
+                in0=a_nat[:, fo : fo + 16].unsqueeze(1).unsqueeze(3).to_broadcast([P, 2, 16, 8]),
+                in1=a_per[:, fo : fo + 16].rearrange("p (w r) -> p w r", r=8).unsqueeze(2).to_broadcast([P, 2, 16, 8]),
+                op=ALU.mult,
+            )
             t_q[k] = q32
 
         def st_sqrt(k):
@@ -332,6 +337,8 @@ def tile_bcnnresnet_t_kernel(tc, feat, W, b, out):
             return 0 <= k < NT
 
         st_sign(0)
+        st_prod_v(0)
+        w_reorder()
         for s in range(NT + 6):
             if on(s):
                 st_prod(s)
@@ -349,6 +356,8 @@ def tile_bcnnresnet_t_kernel(tc, feat, W, b, out):
                 st_out(s - 6, 1)
             if on(s - 4):
                 st_quant(s - 4)
+            if on(s + 1):
+                st_prod_v(s + 1)
             if on(s - 2):
                 st_mirror(s - 2)
             if on(s - 3):

from contextlib import ExitStack

import concourse.mybir as mybir
from concourse.masks import make_identity

F32 = mybir.dt.float32
BF16 = mybir.dt.bfloat16
U32 = mybir.dt.uint32
U8 = mybir.dt.uint8
FP8X4 = mybir.dt.float8_e4m3fn_x4
ALU = mybir.AluOpType
ACTF = mybir.ActivationFunctionType
AX = mybir.AxisListType

P = 128
B, D, C = 4096, 32, 1024
K = D * D
NT = B // P
EPS_SQRT = 1e-10
EPS_NORM = 1e-12
FLOPS = 2 * B * K * C
HEAD = 8


def tile_bcnnresnet_t_kernel(tc, feat, W, b, out):
    nc = tc.nc
    with ExitStack() as ctx:
        ctx.enter_context(tc.manual_schedule())
        keep = ctx.enter_context(tc.tile_pool(name="keep", bufs=1))
        qpool = ctx.enter_context(tc.tile_pool(name="qpool", bufs=4))
        xpool = ctx.enter_context(tc.tile_pool(name="xpool", bufs=5))
        gpool = ctx.enter_context(tc.tile_pool(name="gpool", bufs=3))
        cpool = ctx.enter_context(tc.tile_pool(name="cpool", bufs=3))
        opool = ctx.enter_context(tc.tile_pool(name="opool", bufs=6))
        ps_t = ctx.enter_context(tc.psum_pool(name="ps_t", bufs=2))
        ps_s = ctx.enter_context(tc.psum_pool(name="ps_s", bufs=2))
        ps_o = ctx.enter_context(tc.psum_pool(name="ps_o", bufs=4))

        f_sb = keep.tile([P, NT * D], BF16)
        nc.sync.dma_start(out=f_sb[:], in_=feat.rearrange("(p t) d -> p (t d)", t=NT))
        w_raw = keep.tile([P, 8 * K], BF16)
        w_view = W.rearrange("(ct p) k -> p ct k", p=P)
        for g in range(4):
            nc.sync.dma_start(
                out=w_raw[:, 2 * g * K : (2 * g + 2) * K].rearrange("p (ct k) -> p ct k", ct=2),
                in_=w_view[:, 2 * g : 2 * g + 2, :],
            )
        bias_bf = keep.tile([P, C], BF16)
        nc.sync.dma_start(out=bias_bf[:], in_=b.partition_broadcast(P))

        ident_bf = keep.tile([P, P], BF16)
        make_identity(nc, ident_bf[:])
        ident_f = keep.tile([P, P], F32)
        make_identity(nc, ident_f[:])

        sel_per = keep.tile([P, P], BF16)
        sel_col = keep.tile([P, 4 * 48], BF16)
        sel_row = keep.tile([P, 4 * 384], BF16)

        def sel_small():
            nc.vector.tensor_copy(
                out=sel_per[:].rearrange("p (m e r) -> p m e r", e=2, r=8),
                in_=ident_bf[:].rearrange("p (m r e) -> p m e r", e=2, r=8),
            )
            nc.vector.tensor_copy(
                out=sel_col[:].rearrange("p (a w) -> p a w", a=4)[:, :, 0:32],
                in_=sel_per[:].rearrange("p (a w) -> p a w", a=4),
            )
            nc.vector.tensor_copy(
                out=sel_col[:].rearrange("p (a w) -> p a w", a=4)[:, :, 32:48],
                in_=sel_per[:].rearrange("p (a w) -> p a w", a=4)[:, :, 16:32],
            )

        def sel_big(a, part):
            lo = a * 384
            if part == 0:
                nc.vector.tensor_copy(
                    out=sel_row[:, lo : lo + 256].rearrange("p (z q r) -> p z q r", z=2, r=8),
                    in_=ident_bf[:, 32 * a : 32 * a + 16].unsqueeze(1).unsqueeze(3).to_broadcast([P, 2, 16, 8]),
                )
            else:
                nc.vector.tensor_copy(
                    out=sel_row[:, lo + 256 : lo + 384].rearrange("p (q r) -> p q r", r=8),
                    in_=ident_bf[:, 32 * a + 16 : 32 * a + 32].unsqueeze(2).to_broadcast([P, 16, 8]),
                )

        a_nat = keep.tile([P, NT * D], F32)
        a_per = keep.tile([P, NT * D], F32)
        s_nat = keep.tile([P, NT * D], BF16)
        nz = keep.tile([P, NT * D], BF16)
        cnt = keep.tile([P, NT], F32)
        sq_c = keep.tile([P, NT], F32)
        sum_a = keep.tile([P, NT], F32)
        sq_a = keep.tile([P, NT], F32)
        n2 = keep.tile([P, NT], F32)
        n2c = keep.tile([P, NT], F32)
        rho = keep.tile([P, NT], F32)
        erho = keep.tile([P, NT], F32)
        s_t = keep.tile([P, 8, P], BF16)

        def scalar_prep(t0, t1):
            lo, hi = t0 * D, t1 * D
            nc.scalar.activation(out=a_nat[:, lo:hi], in_=f_sb[:, lo:hi], func=ACTF.Abs)
            nc.scalar.activation(
                out=a_per[:, lo:hi].rearrange("p (m e r) -> p m e r", e=2, r=8),
                in_=f_sb[:, lo:hi].rearrange("p (m r e) -> p m e r", e=2, r=8),
                func=ACTF.Abs,
            )
            nc.scalar.activation(out=s_nat[:, lo:hi], in_=f_sb[:, lo:hi], func=ACTF.Sign)

        def vector_prep(t0, t1):
            lo, hi = t0 * D, t1 * D
            ts = slice(t0, t1)
            return [
                lambda: nc.vector.tensor_single_scalar(
                    out=nz[:, lo:hi], in_=f_sb[:, lo:hi], scalar=0.0, op=ALU.not_equal
                ),
                lambda: nc.vector.tensor_reduce(
                    out=cnt[:, ts], in_=nz[:, lo:hi].rearrange("p (t d) -> p t d", d=D), axis=AX.X, op=ALU.add
                ),
                lambda: nc.vector.tensor_reduce(
                    out=sum_a[:, ts], in_=a_nat[:, lo:hi].rearrange("p (t d) -> p t d", d=D), axis=AX.X, op=ALU.add
                ),
                lambda: nc.vector.tensor_tensor(out=sq_c[:, ts], in0=cnt[:, ts], in1=cnt[:, ts], op=ALU.mult),
                lambda: nc.vector.tensor_tensor(out=sq_a[:, ts], in0=sum_a[:, ts], in1=sum_a[:, ts], op=ALU.mult),
                lambda: nc.vector.scalar_tensor_tensor(
                    out=n2[:, ts], in0=sq_c[:, ts], scalar=EPS_SQRT, in1=sq_a[:, ts], op0=ALU.mult, op1=ALU.add
                ),
                lambda: nc.vector.tensor_scalar_max(out=n2c[:, ts], in0=n2[:, ts], scalar1=EPS_NORM * EPS_NORM),
                lambda: nc.vector.reciprocal(out=rho[:, ts], in_=n2c[:, ts]),
                lambda: nc.vector.tensor_scalar_mul(out=erho[:, ts], in0=rho[:, ts], scalar1=EPS_SQRT),
            ]

        def sign_rows(g0, g1):
            st_ps = ps_t.tile([P, 8, P], BF16, tag="tp")
            for g in range(g0, g1):
                nc.tensor.transpose(
                    out=st_ps[:, g, :], in_=s_nat[:, g * P : (g + 1) * P], identity=ident_bf[:]
                )
            nc.scalar.copy(out=s_t[:, g0:g1, :], in_=st_ps[:, g0:g1, :])

        sel_small()
        sel_big(0, 0)
        sel_big(0, 1)
        scalar_prep(0, HEAD)
        scalar_prep(HEAD, NT)
        first, rest = vector_prep(0, HEAD), vector_prep(HEAD, NT)
        fill = [(a, part) for a in range(1, 4) for part in range(2)]
        first[0]()
        rest[0]()
        first[1]()
        first[2]()
        sel_big(*fill[0])
        first[3]()
        first[4]()
        sel_big(*fill[1])
        sel_big(*fill[2])
        first[5]()
        rest[1]()
        first[6]()
        rest[2]()
        first[7]()
        sel_big(*fill[3])
        sel_big(*fill[4])
        sel_big(*fill[5])
        first[8]()
        for step in rest[3:]:
            step()
        sign_rows(0, HEAD // 4)

        w_ord = keep.tile([P, 8 * K], BF16)
        w_grp = keep.tile([P, 2 * C * 4], BF16, align_bytes=64)
        w_cod = keep.tile([P, 2 * C], U32, align_bytes=64)
        w_scl = keep.tile([P, 2 * C], U8, align_bytes=64)
        raw_w = w_raw[:].bitcast(F32)
        ord_w = w_ord[:].bitcast(F32)
        grp_w = w_grp[:].bitcast(F32).rearrange("p (c n u) -> p c n u", c=2, u=2)

        def w_reorder():
            for ct in range(8):
                for c in range(2):
                    lo = ct * 512 + c * 256
                    nc.vector.tensor_copy(
                        out=ord_w[:, lo : lo + 256].rearrange("p (u q r) -> p u q r", u=2, r=8),
                        in_=raw_w[:, lo : lo + 256].rearrange("p (q u r) -> p u q r", u=2, r=8),
                    )

        def w_stage(ct):
            wt = ps_t.tile([P, 4, P], F32, tag="tp")
            for s in range(4):
                lo = ct * 512 + s * 128
                nc.tensor.transpose(out=wt[:, s, :], in_=ord_w[:, lo : lo + 128], identity=ident_f[:])
            nc.scalar.copy(
                out=grp_w[:, :, ct * P : (ct + 1) * P, :],
                in_=wt[:].rearrange("p (c u) n -> p c n u", c=2),
            )
            if ct % 4 == 3:
                h = ct // 4
                for c in range(2):
                    lo = c * C + h * 512
                    nc.vector.quantize_mx(
                        out=w_cod[:, lo : lo + 512].bitcast(FP8X4),
                        scales=w_scl[:, lo : lo + 512],
                        in_=w_grp[:, 4 * lo : 4 * lo + 2048],
                    )

        out_v = out.rearrange("(p t) c -> p t c", t=NT)
        t_q, t_x, t_sg, t_xt, t_g, t_c, t_acc, t_o = {}, {}, {}, {}, {}, {}, {}, {}

        def st_sign(kp):
            g, hh = kp // 2, kp % 2
            sg = ps_s.tile([P, 1024], BF16)
            for kk in range(2):
                a = 2 * hh + kk
                nc.tensor.matmul(
                    out=sg[:, kk * 384 : (kk + 1) * 384],
                    lhsT=s_t[:, g, :],
                    rhs=sel_row[:, a * 384 : (a + 1) * 384],
                    start=True,
                    stop=True,
                )
            nc.tensor.matmul(
                out=sg[:, 768:864], lhsT=s_t[:, g, :], rhs=sel_col[:, hh * 96 : (hh + 1) * 96], start=True, stop=True
            )
            t_sg[kp] = sg

        def st_prod(k):
            fo = k * D
            nc.gpsimd.tensor_tensor(
                out=t_q[k][:, 0:512].rearrange("p (w q r) -> p w q r", w=4, r=8),
                in0=a_nat[:, fo : fo + 16].unsqueeze(1).unsqueeze(3).to_broadcast([P, 4, 16, 8]),
                in1=a_per[:, fo : fo + 32].rearrange("p (w r) -> p w r", r=8).unsqueeze(2).to_broadcast([P, 4, 16, 8]),
                op=ALU.mult,
            )

        def st_prod_v(k):
            fo = k * D + 16
            q32 = qpool.tile([P, 768], F32)
            nc.vector.tensor_tensor(
                out=q32[:, 512:768].rearrange("p (w q r) -> p w q r", w=2, r=8),
                in0=a_nat[:, fo : fo + 16].unsqueeze(1).unsqueeze(3).to_broadcast([P, 2, 16, 8]),
                in1=a_per[:, fo : fo + 16].rearrange("p (w r) -> p w r", r=8).unsqueeze(2).to_broadcast([P, 2, 16, 8]),
                op=ALU.mult,
            )
            t_q[k] = q32

        def st_sqrt(k):
            xf = xpool.tile([P, K], BF16)
            nc.scalar.activation(
                out=xf[:, 0:768], in_=t_q[k][:], func=ACTF.Sqrt, bias=erho[:, k : k + 1], scale=rho[:, k : k + 1]
            )
            t_x[k] = xf

        def st_sign_col(k):
            xf, sg = t_x[k], t_sg[k // 2]
            so = 768 + (k % 2) * 48
            nc.vector.tensor_tensor(
                out=xf[:, 0:768].rearrange("p (w q r) -> p w q r", w=6, r=8),
                in0=xf[:, 0:768].rearrange("p (w q r) -> p w q r", w=6, r=8),
                in1=sg[:, so : so + 48].rearrange("p (w r) -> p w r", r=8).unsqueeze(2).to_broadcast([P, 6, 16, 8]),
                op=ALU.mult,
            )

        def st_sign_row(k):
            xf, sg = t_x[k], t_sg[k // 2]
            ro = (k % 2) * 384
            nc.vector.tensor_tensor(
                out=xf[:, 0:768].rearrange("p (z e m) -> p z e m", z=3, e=2),
                in0=xf[:, 0:768].rearrange("p (z e m) -> p z e m", z=3, e=2),
                in1=sg[:, ro : ro + 384].rearrange("p (z m) -> p z m", z=3).unsqueeze(2).to_broadcast([P, 3, 2, 128]),
                op=ALU.mult,
            )

        def st_mirror(k):
            xf = t_x[k]
            for eb in range(2):
                nc.scalar.copy(
                    out=xf[:, 768 + 128 * eb : 896 + 128 * eb].rearrange("p (ra ea rb) -> p ra ea rb", ra=8, ea=2),
                    in_=xf[:, 256:512].rearrange("p (ea rb eb ra) -> p eb ra ea rb", ea=2, rb=8, eb=2)[:, eb],
                )

        def st_transpose(k):
            xf = t_x[k]
            xt = ps_t.tile([P, 8, P], BF16, tag="tp")
            for c, u, z in ((0, 0, 0), (0, 1, 1), (1, 0, 3), (1, 1, 2)):
                for e in range(2):
                    lo = z * 256 + e * 128
                    nc.tensor.transpose(
                        out=xt[:, 4 * c + 2 * u + e, :], in_=xf[:, lo : lo + 128], identity=ident_bf[:]
                    )
            t_xt[k] = xt

        def st_group(k):
            grp = gpool.tile([P, K], BF16, align_bytes=64)
            nc.scalar.copy(
                out=grp[:].rearrange("p (c n t) -> p c n t", c=2, t=4),
                in_=t_xt[k][:].rearrange("p (c t) n -> p c n t", c=2),
            )
            t_g[k] = grp

        def st_quant(k):
            x_cod = cpool.tile([P, 256], U32, align_bytes=64)
            x_scl = cpool.tile([P, 256], U8, align_bytes=64)
            nc.vector.quantize_mx(out=x_cod[:].bitcast(FP8X4), scales=x_scl[:], in_=t_g[k][:])
            t_c[k] = (x_cod, x_scl)

        def st_mx(k):
            x_cod, x_scl = t_c[k]
            for h in range(2):
                acc = ps_o.tile([P, 512], F32)
                for c in range(2):
                    lo = c * C + h * 512
                    nc.tensor.matmul_mx(
                        out=acc[:],
                        lhsT=x_cod[:, c * P : (c + 1) * P].bitcast(FP8X4),
                        lhsT_scale=x_scl[:, c * P : (c + 1) * P],
                        rhs=w_cod[:, lo : lo + 512].bitcast(FP8X4),
                        rhs_scale=w_scl[:, lo : lo + 512],
                        start=(c == 0),
                        stop=(c == 1),
                    )
                t_acc[(k, h)] = acc

        def st_out(k, h):
            if h == 0:
                o_new = opool.tile([P, C], F32, name="o_sb")
                t_o[k] = o_new
            o_sb = t_o[k]
            cols = slice(h * 512, (h + 1) * 512)
            nc.vector.tensor_tensor(out=o_sb[:, cols], in0=t_acc[(k, h)][:], in1=bias_bf[:, cols], op=ALU.add)
            if k == NT - 1:
                nc.sync.dma_start(out=out_v[:, k, cols], in_=o_sb[:, cols])
            elif h == 1:
                nc.sync.dma_start(out=out_v[:, k, :], in_=o_sb[:])

        def on(k):
            return 0 <= k < NT

        st_sign(0)
        st_prod_v(0)
        w_reorder()
        for s in range(NT + 6):
            if on(s):
                st_prod(s)
            if on(s - 1):
                st_sqrt(s - 1)
            if on(s - 3):
                st_transpose(s - 3)
            if on(s - 2):
                st_sign_col(s - 2)
            if on(s - 6):
                st_out(s - 6, 0)
            if on(s - 2):
                st_sign_row(s - 2)
            if on(s - 6):
                st_out(s - 6, 1)
            if on(s - 4):
                st_quant(s - 4)
            if on(s + 1):
                st_prod_v(s + 1)
            if on(s - 2):
                st_mirror(s - 2)
            if on(s - 3):
                st_group(s - 3)
            if on(s - 5):
                st_mx(s - 5)
            if s % 2 == 1 and on(s + 1):
                st_sign((s + 1) // 2)
            for ct in range(3 * s, min(3 * s + 3, 8)):
                w_stage(ct)
            if s == 1:
                sign_rows(HEAD // 4, 8)
